import numpy as np
import ml_dtypes


def mxq(x, axis, fmt="e4m3"):
    dtype, down = {"e4m3": (ml_dtypes.float8_e4m3fn, 7), "e5m2": (ml_dtypes.float8_e5m2, 14)}[fmt]
    v = np.moveaxis(np.asarray(x, np.float32).astype(ml_dtypes.bfloat16).astype(np.float64), axis, -1)
    blocks = v.reshape(v.shape[:-1] + (-1, 32))
    amax = np.abs(blocks).max(-1, keepdims=True)
    byte = np.maximum(np.where(amax > 0, np.frexp(amax)[1] - 1 + 127, 0) - down, 1)
    scale = np.exp2(byte - 127.0)
    codes = (blocks / scale).astype(np.float32).astype(dtype).astype(np.float64)
    return np.moveaxis((codes * scale).reshape(v.shape), -1, axis)


WIDE = False


def mx_kscale(k):
    if not WIDE:
        return np.ones(k)
    levels = np.array([10, -10, 5, -5, 0])
    if k % 512:
        return np.exp2(np.random.permutation(np.resize(levels, k // 32))).repeat(32)
    a = np.empty((k // 512, 16))
    for p in range(k // 512):
        a[p, :8] = np.random.permutation(np.resize(levels, 8))
        for g in range(8):
            far = levels[np.abs(levels - a[p, g]) >= 10]
            a[p, g + 8] = far[np.random.randint(len(far))]
    return np.exp2(a.ravel()).repeat(32)


BF16 = ml_dtypes.bfloat16


def bf(x):
    return np.asarray(x, np.float32).astype(BF16)


def f64(x):
    return np.asarray(x).astype(np.float64)


B, H, W, C, NF, ZD = 128, 4, 4, 512, 512, 512
EPS = 1e-8
LRELU_SLOPE = 0.2


def draw0():
    s = mx_kscale(C)
    return {"x": bf(np.random.standard_normal((B, H, W, C)) * s),
            "dlatents": bf(np.random.standard_normal((B, ZD))),
            "noise_map": bf(np.random.standard_normal((B, H, W, 1))),
            "conv_w": bf(np.random.standard_normal((C, NF)) / np.sqrt(C) / s[:, None]),
            "noise_weight": bf(np.random.standard_normal((1, 1, 1, NF)) * 0.5),
            "bias": bf(np.random.standard_normal((1, 1, 1, NF)) * 0.5),
            "dense_w": bf(np.random.standard_normal((ZD, 2 * NF)) / np.sqrt(ZD)),
            "dense_b": bf(np.random.standard_normal(2 * NF) * 0.3)}


def core(x, dlatents, noise_map, conv_w, noise_weight, bias, dense_w, dense_b):
    y = mxq(f64(x), 3, "e4m3") @ mxq(f64(conv_w), 0, "e4m3")
    y = y + f64(noise_weight) * f64(noise_map) + f64(bias)
    y = np.where(y >= 0.0, y, LRELU_SLOPE * y)
    mu = np.mean(y, axis=(1, 2), keepdims=True)
    var = np.mean(np.square(y - mu), axis=(1, 2), keepdims=True)
    yn = (y - mu) / np.sqrt(var + EPS)
    gb = f64(dlatents) @ f64(dense_w) + f64(dense_b)
    nf = y.shape[-1]
    gb = gb.reshape(-1, 2, 1, 1, nf)
    gamma, beta = gb[:, 0], gb[:, 1]
    return yn * (1.0 + gamma) + beta


def e4m3fn_bytes(y):
    return np.clip(np.asarray(y, np.float64), -448.0, 448.0).astype(np.float32).astype(ml_dtypes.float8_e4m3fn).view(np.uint8)


def e4m3fn_values(b):
    return np.asarray(b, np.uint8).view(ml_dtypes.float8_e4m3fn).astype(np.float64)


def setup_inputs():
    d = draw0()
    x0 = np.asarray(d['x']).astype(np.float64)
    s = (np.max(np.abs(x0), axis=(0, 1, 2), keepdims=True) / 448.0).astype(np.float32)
    out = {}
    for k, v in d.items():
        if k == 'x':
            out['x_bytes'] = e4m3fn_bytes(x0 / s.astype(np.float64))
            out['x_scale'] = s
        else:
            out[k] = v
    return out


def reference(x_bytes, x_scale, dlatents, noise_map, conv_w, noise_weight, bias, dense_w, dense_b):
    return core(e4m3fn_values(x_bytes) * x_scale.astype(np.float64), dlatents, noise_map, conv_w, noise_weight, bias, dense_w, dense_b)

@@ -1,0 +1,470 @@
+from contextlib import ExitStack
+
+import concourse.mybir as mybir
+from concourse.masks import make_identity
+
+F32 = mybir.dt.float32
+BF16 = mybir.dt.bfloat16
+U32 = mybir.dt.uint32
+U8 = mybir.dt.uint8
+FP8 = mybir.dt.float8_e4m3fn
+FP8X4 = mybir.dt.float8_e4m3fn_x4
+ALU = mybir.AluOpType
+ACT = mybir.ActivationFunctionType
+
+P = 128
+PIX = 16
+K = 512
+PACK = 4
+NF = 512
+TILES = NF // P
+PAIRS = TILES // 2
+CHUNK_PIX = 4
+CHUNKS = PIX // CHUNK_PIX
+CHUNK = CHUNK_PIX * P
+STEPS = PAIRS * CHUNKS
+HALF_PIX = PIX // 2
+DENSE_KT = 4
+ROW_NOISE_WEIGHT, ROW_BIAS, ROW_DENSE_GAMMA, ROW_DENSE_BETA, ROWS = 0, 4, 8, 12, 16
+EPS = 1e-8
+SLOPE = 0.2
+
+FLOPS = 2 * P * PIX * K * NF + 2 * P * 512 * 2 * NF
+
+
+def tile_styleganlayerepilogue_kernel(
+    tc, x_bytes, x_scale, dlatents, noise_map, conv_w, noise_weight, bias, dense_w, dense_b, out
+):
+    nc = tc.nc
+    with ExitStack() as ctx:
+        const = ctx.enter_context(tc.tile_pool(name="const", bufs=1))
+        xs_pool = ctx.enter_context(tc.tile_pool(name="xs_pool", bufs=6))
+        grouped_pool = ctx.enter_context(tc.tile_pool(name="grouped_pool", bufs=CHUNKS))
+        z_pool = ctx.enter_context(tc.tile_pool(name="z_pool", bufs=3))
+        q_pool = ctx.enter_context(tc.tile_pool(name="q_pool", bufs=3))
+        stat_pool = ctx.enter_context(tc.tile_pool(name="stat_pool", bufs=PAIRS))
+        ya_pool = ctx.enter_context(tc.tile_pool(name="ya_pool", bufs=5))
+        o_pool = ctx.enter_context(tc.tile_pool(name="o_pool", bufs=6))
+        psum = ctx.enter_context(tc.psum_pool(name="psum", bufs=2))
+        ctx.enter_context(tc.manual_schedule())
+
+        def work_bank(shape, dtype, name):
+            return psum.tile(shape, dtype, tag="work", bufs=5, name=name)
+
+        def held_bank(shape, dtype, name):
+            return psum.tile(shape, dtype, tag="held", bufs=3, name=name)
+
+        neg_eps = const.tile([P, 1], F32, name="neg_eps")
+        nc.vector.memset(neg_eps[:], -EPS)
+        vec_rows = const.tile([P, P], BF16, name="vec_rows")
+        nc.vector.memset(vec_rows[:], 0.0)
+
+        scale_bc = const.tile([P, K], F32, name="scale_bc")
+        nc.sync.dma_start(
+            out=scale_bc[:], in_=x_scale.rearrange("a b c k -> (a b c k)").partition_broadcast(P)
+        )
+        noise_sb = const.tile([P, PIX], BF16, name="noise_sb")
+        nc.scalar.dma_start(out=noise_sb[:], in_=noise_map.rearrange("b h w o -> b (h w o)"))
+        nc.scalar.dma_start(
+            out=vec_rows[ROW_NOISE_WEIGHT:ROW_BIAS, :], in_=noise_weight.rearrange("a b c (t p) -> (a b c t) p", p=P)
+        )
+        nc.scalar.dma_start(
+            out=vec_rows[ROW_BIAS:ROW_DENSE_GAMMA, :], in_=bias.rearrange("a b c (t p) -> (a b c t) p", p=P)
+        )
+        nc.scalar.dma_start(out=vec_rows[ROW_DENSE_GAMMA:ROWS, :], in_=dense_b.rearrange("(t p) -> t p", p=P))
+        warm = const.tile([P, 1], F32, name="warm")
+        nc.scalar.activation(out=warm[:], in_=neg_eps[:], func=ACT.Abs_reciprocal_sqrt)
+
+        x_src = x_bytes.rearrange("b h w k -> b (h w) k")
+        w_raw = const.tile([P, PACK, NF], BF16, name="w_raw")
+        dl_sb = const.tile([P, DENSE_KT * P], BF16, name="dl_sb")
+        dense_w_sb = const.tile([P, DENSE_KT, 2 * NF], BF16, name="dense_w_sb")
+        x_byte_tiles = []
+        for i in range(PIX // 2):
+            x_byte_tile = const.tile([P, 2, K], U8, name="xbytes%d" % i)
+            nc.sync.dma_start(out=x_byte_tile[:], in_=x_src[:, 2 * i : 2 * i + 2, :])
+            x_byte_tiles.append(x_byte_tile)
+            if 2 * (i + 1) == 2 * CHUNK_PIX:
+                nc.sync.dma_start(out=w_raw[:], in_=conv_w.rearrange("(p j) o -> p j o", j=PACK))
+        nc.sync.dma_start(out=dl_sb[:], in_=dlatents)
+        nc.sync.dma_start(out=dense_w_sb[:], in_=dense_w.rearrange("(t p) n -> p t n", p=P))
+
+        ident_b = const.tile([P, P], BF16, name="ident_b")
+        make_identity(nc, ident_b[:])
+        ident_f = const.tile([P, P], F32, name="ident_f")
+        make_identity(nc, ident_f[:])
+
+        def transpose_add(dst, src, start, stop):
+            nc.tensor.matmul(out=dst, lhsT=src, rhs=ident_f[:], is_transpose=True, start=start, stop=stop)
+
+        tiles = {}
+
+        vecs = const.tile([P, ROWS], F32, name="vecs")
+        gamma_bias = const.tile([P, TILES], F32, name="gamma_bias")
+        noise_bias = [const.tile([P, PIX * P], F32, name="noise_bias%d" % t) for t in range(TILES)]
+
+        def small_transposes():
+            tiles["vecs_ps"] = work_bank([P, P], BF16, "vecs_ps")
+            nc.tensor.transpose(tiles["vecs_ps"][:], vec_rows[:], ident_b[:])
+            for half in range(2):
+                noise_rows = held_bank([P, HALF_PIX * P], BF16, "noise_rows")
+                for x in range(HALF_PIX):
+                    pix = HALF_PIX * half + x
+                    nc.tensor.transpose(
+                        noise_rows[:, x * P : (x + 1) * P], noise_sb[:, pix : pix + 1].to_broadcast([P, P]), ident_b[:]
+                    )
+                tiles[("noise_rows", half)] = noise_rows
+
+        def small_copies():
+            nc.vector.tensor_copy(out=vecs[:], in_=tiles["vecs_ps"][:, 0:ROWS])
+            nc.vector.tensor_scalar_add(
+                out=gamma_bias[:], in0=vecs[:, ROW_DENSE_GAMMA : ROW_DENSE_GAMMA + TILES], scalar1=1.0
+            )
+
+        def make_noise_bias(t, half):
+            nc.scalar.activation(
+                out=noise_bias[t][:, half * HALF_PIX * P : (half + 1) * HALF_PIX * P],
+                in_=tiles[("noise_rows", half)][:],
+                func=ACT.Identity,
+                bias=vecs[:, ROW_BIAS + t : ROW_BIAS + t + 1],
+                scale=vecs[:, ROW_NOISE_WEIGHT + t : ROW_NOISE_WEIGHT + t + 1],
+            )
+
+        w_grouped = const.tile([P, NF, PACK], BF16, name="w_grouped", align_bytes=64)
+        w_codes = const.tile([P, NF], U32, name="w_codes", align_bytes=64)
+        w_scales = const.tile([P, NF], U8, name="w_scales", align_bytes=64)
+
+        def w_interleave():
+            nc.scalar.copy(out=w_grouped[:], in_=w_raw[:].rearrange("p j o -> p o j"))
+
+        def w_quantize():
+            nc.vector.quantize_mx(
+                out=w_codes[:].bitcast(FP8X4), scales=w_scales[:], in_=w_grouped[:].rearrange("p o j -> p (o j)")
+            )
+
+        def widen(ch, x):
+            pix = ch * CHUNK_PIX + x
+            xs = xs_pool.tile([P, K], BF16, name="xs")
+            nc.vector.tensor_tensor(
+                out=xs[:], in0=x_byte_tiles[pix // 2][:, pix % 2, :].bitcast(FP8), in1=scale_bc[:], op=ALU.mult
+            )
+            tiles[("xs", ch, x)] = xs
+
+        def x_transpose(ch, x):
+            if x % 2 == 0:
+                tiles[("xt", ch, x // 2)] = work_bank([P, 2, 2, P], F32, "xt")
+            words = tiles[("xs", ch, x)][:].bitcast(F32)
+            for u in range(2):
+                nc.tensor.transpose(tiles[("xt", ch, x // 2)][:, x % 2, u, :], words[:, u : K // 2 : 2], ident_f[:])
+
+        def x_group(ch, half):
+            if half == 0:
+                tiles[("grouped", ch)] = grouped_pool.tile([P, CHUNK * PACK], BF16, name="grouped", align_bytes=64)
+            words = tiles[("grouped", ch)][:].bitcast(F32)
+            nc.scalar.copy(
+                out=words[:, half * CHUNK : (half + 1) * CHUNK].rearrange("p (x b u) -> p x b u", x=2, u=2),
+                in_=tiles[("xt", ch, half)][:].rearrange("p x u b -> p x b u"),
+            )
+
+        def x_quantize(ch):
+            codes = const.tile([P, CHUNK], U32, name="x_codes%d" % ch, align_bytes=64)
+            scales = const.tile([P, CHUNK], U8, name="x_scales%d" % ch, align_bytes=64)
+            nc.vector.quantize_mx(out=codes[:].bitcast(FP8X4), scales=scales[:], in_=tiles[("grouped", ch)][:])
+            tiles[("x_codes", ch)] = codes
+            tiles[("x_scales", ch)] = scales
+
+        dlatents_t = const.tile([P, DENSE_KT, P], BF16, name="dlatents_t")
+        gamma1 = const.tile([P, TILES, P], F32, name="gamma1")
+        beta = const.tile([P, TILES, P], F32, name="beta")
+
+        def dlatents_transpose():
+            tiles["dlatents_ps"] = work_bank([P, DENSE_KT, P], BF16, "dlatents_ps")
+            for kt in range(DENSE_KT):
+                nc.tensor.transpose(tiles["dlatents_ps"][:, kt, :], dl_sb[:, kt * P : (kt + 1) * P], ident_b[:])
+
+        def dlatents_copy():
+            nc.scalar.copy(out=dlatents_t[:], in_=tiles["dlatents_ps"][:])
+
+        def dense_matmul(part):
+            dense_ps = work_bank([P, TILES, P], F32, "dense_ps")
+            for t in range(TILES):
+                col = (part * TILES + t) * P
+                for kt in range(DENSE_KT):
+                    nc.tensor.matmul(
+                        out=dense_ps[:, t, :],
+                        lhsT=dense_w_sb[:, kt, col : col + P],
+                        rhs=dlatents_t[:, kt, :],
+                        start=(kt == 0),
+                        stop=(kt == DENSE_KT - 1),
+                    )
+            tiles[("dense_ps", part)] = dense_ps
+
+        def dense_bias(part):
+            for t in range(TILES):
+                nc.scalar.activation(
+                    out=(gamma1 if part == 0 else beta)[:, t, :],
+                    in_=tiles[("dense_ps", part)][:, t, :],
+                    func=ACT.Identity,
+                    bias=(gamma_bias if part == 0 else vecs[:, ROW_DENSE_BETA:ROWS])[:, t : t + 1],
+                    scale=1.0,
+                )
+
+        def conv(s):
+            g, ch = s // CHUNKS, s % CHUNKS
+            for c in range(2):
+                t = 2 * g + c
+                acc = work_bank([P, CHUNK], F32, "acc")
+                nc.tensor.matmul_mx(
+                    out=acc[:],
+                    lhsT=w_codes[:, t * P : (t + 1) * P].bitcast(FP8X4),
+                    lhsT_scale=w_scales[:, t * P : (t + 1) * P],
+                    rhs=tiles[("x_codes", ch)][:].bitcast(FP8X4),
+                    rhs_scale=tiles[("x_scales", ch)][:],
+                    start=True,
+                    stop=True,
+                )
+                tiles[("acc", s, c)] = acc
+
+        def add_noise(s):
+            g, ch = s // CHUNKS, s % CHUNKS
+            z = z_pool.tile([P, 2, CHUNK], F32, name="z")
+            for c in range(2):
+                nc.vector.tensor_tensor(
+                    out=z[:, c, :],
+                    in0=tiles[("acc", s, c)][:],
+                    in1=noise_bias[2 * g + c][:, ch * CHUNK : (ch + 1) * CHUNK],
+                    op=ALU.add,
+                )
+            tiles[("z", s)] = z
+
+        def leaky_relu(s):
+            y = const.tile([P, 2, CHUNK_PIX, P], F32, name="y%d" % s)
+            z = tiles[("z", s)][:].rearrange("p c n -> p (c n)")
+            nc.vector.scalar_tensor_tensor(
+                out=y[:].rearrange("p c x b -> p (c x b)"), in0=z, scalar=SLOPE, in1=z, op0=ALU.mult, op1=ALU.max
+            )
+            tiles[("y", s)] = y
+
+        def square(s):
+            q = q_pool.tile([P, 2, CHUNK_PIX, P], F32, name="q")
+            nc.scalar.activation(
+                out=q[:].rearrange("p c x b -> p (c x b)"),
+                in_=tiles[("y", s)][:].rearrange("p c x b -> p (c x b)"),
+                func=ACT.Square,
+            )
+            tiles[("q", s)] = q
+
+        def sum_pixels(s, power):
+            g, ch = s // CHUNKS, s % CHUNKS
+            if ch == 0 and power == 0:
+                tiles[("sums", g)] = held_bank([P, 2, 2, P], F32, "sums")
+            src = tiles[("y" if power == 0 else "q", s)]
+            for c in range(2):
+                for x in range(CHUNK_PIX):
+                    transpose_add(
+                        tiles[("sums", g)][:, c, power, :],
+                        src[:, c, x, :],
+                        ch == 0 and power == 0 and c == 0 and x == 0,
+                        ch == CHUNKS - 1 and power == 1 and c == 1 and x == CHUNK_PIX - 1,
+                    )
+
+        def stats_out(g):
+            sums = tiles[("sums", g)]
+            parts = stat_pool.tile([P, 2, 3, P], F32, name="parts")
+            nc.scalar.copy(out=parts[:, :, 0, :], in_=sums[:, :, 0, :])
+            nc.scalar.activation(out=parts[:, :, 1, :], in_=sums[:, :, 1, :], func=ACT.Copy, scale=-1.0 / PIX)
+            nc.scalar.activation(out=parts[:, :, 2, :], in_=sums[:, :, 0, :], func=ACT.Square, scale=1.0 / PIX)
+            tiles[("parts", g)] = parts
+
+        def stats_back(g):
+            parts = tiles[("parts", g)]
+            stats = held_bank([P, 2, 2, P], F32, "stats")
+            for c in range(2):
+                transpose_add(stats[:, c, 0, :], parts[:, c, 0, :], c == 0, False)
+                transpose_add(stats[:, c, 1, :], parts[:, c, 1, :], False, False)
+                transpose_add(stats[:, c, 1, :], parts[:, c, 2, :], False, c == 1)
+            tiles[("stats", g)] = stats
+
+        def stats_rstd(g):
+            rstd = stat_pool.tile([P, 2, P], F32, name="rstd")
+            nc.scalar.activation(
+                out=rstd[:],
+                in_=tiles[("stats", g)][:, :, 1, :],
+                func=ACT.Abs_reciprocal_sqrt,
+                bias=neg_eps[:],
+                scale=1.0,
+            )
+            tiles[("rstd", g)] = rstd
+
+        def make_gain(g):
+            gain = stat_pool.tile([P, 2, 1, P], F32, name="gain")
+            nc.vector.tensor_tensor(
+                out=gain[:, :, 0, :], in0=gamma1[:, 2 * g : 2 * g + 2, :], in1=tiles[("rstd", g)][:], op=ALU.mult
+            )
+            tiles[("gain", g)] = gain
+
+        def make_mean_term(g):
+            mean_term = stat_pool.tile([P, 2, P], F32, name="mean_term")
+            nc.vector.scalar_tensor_tensor(
+                out=mean_term[:],
+                in0=tiles[("stats", g)][:, :, 0, :],
+                scalar=-1.0 / PIX,
+                in1=tiles[("gain", g)][:, :, 0, :],
+                op0=ALU.mult,
+                op1=ALU.mult,
+            )
+            tiles[("mean_term", g)] = mean_term
+
+        def make_shift(g):
+            shift = stat_pool.tile([P, 2, P], F32, name="shift")
+            nc.vector.tensor_tensor(
+                out=shift[:], in0=tiles[("mean_term", g)][:], in1=beta[:, 2 * g : 2 * g + 2, :], op=ALU.add
+            )
+            tiles[("shift", g)] = shift
+
+        out_v = out.rearrange("b h w o -> b (h w) o")
+
+        def scale_y(g, ch):
+            ya = ya_pool.tile([P, 2, CHUNK_PIX, P], F32, name="ya")
+            nc.vector.tensor_tensor(
+                out=ya[:],
+                in0=tiles[("y", g * CHUNKS + ch)][:],
+                in1=tiles[("gain", g)][:].to_broadcast([P, 2, CHUNK_PIX, P]),
+                op=ALU.mult,
+            )
+            tiles[("ya", g, ch)] = ya
+
+        def out_shift(g, ch, half):
+            out_ps = work_bank([P, 2, 2, P], F32, "out_ps")
+            for x in range(2):
+                for c in range(2):
+                    transpose_add(out_ps[:, x, c, :], tiles[("shift", g)][:, c, :], x == 0 and c == 0, False)
+            tiles[("out_ps", g, ch, half)] = out_ps
+
+        def out_product(g, ch, half):
+            for x in range(2):
+                for c in range(2):
+                    transpose_add(
+                        tiles[("out_ps", g, ch, half)][:, x, c, :],
+                        tiles[("ya", g, ch)][:, c, 2 * half + x, :],
+                        False,
+                        x == 1 and c == 1,
+                    )
+
+        def out_copy(g, ch, half):
+            if half == 0:
+                tiles[("out_sb", g, ch)] = o_pool.tile([P, CHUNK_PIX, 2, P], F32, name="out_sb")
+            nc.scalar.copy(
+                out=tiles[("out_sb", g, ch)][:, 2 * half : 2 * half + 2, :, :], in_=tiles[("out_ps", g, ch, half)][:]
+            )
+
+        def store(g, ch, first, count):
+            nc.sync.dma_start(
+                out=out_v[:, ch * CHUNK_PIX + first : ch * CHUNK_PIX + first + count, g * 2 * P : (g + 1) * 2 * P],
+                in_=tiles[("out_sb", g, ch)][:, first : first + count, :, :].rearrange("p x c o -> p x (c o)"),
+            )
+
+        def front(ch, pixels):
+            for x in pixels:
+                widen(ch, x)
+                x_transpose(ch, x)
+                if x % 2 == 1:
+                    x_group(ch, x // 2)
+
+        def turn_out(g, ch):
+            out_shift(g, ch, 0)
+            out_shift(g, ch, 1)
+            out_product(g, ch, 0)
+            out_product(g, ch, 1)
+
+        small_transposes()
+        small_copies()
+        make_noise_bias(0, 0)
+        make_noise_bias(1, 0)
+        w_interleave()
+        front(0, range(4))
+        dlatents_transpose()
+        front(1, range(2))
+        dlatents_copy()
+        make_noise_bias(0, 1)
+        front(1, range(2, 4))
+        make_noise_bias(1, 1)
+        front(2, range(4))
+        dense_matmul(0)
+        dense_bias(0)
+        front(3, range(2))
+        w_quantize()
+        x_quantize(0)
+        front(3, range(2, 4))
+        x_quantize(1)
+        x_quantize(2)
+        conv(0)
+        dense_matmul(1)
+        dense_bias(1)
+        conv(1)
+        make_noise_bias(2, 0)
+        make_noise_bias(3, 0)
+
+        pair_0_summed = CHUNKS + 1
+        for i in range(STEPS + 1):
+            if i < STEPS:
+                add_noise(i)
+            if i == 0:
+                x_quantize(CHUNKS - 1)
+            if i == STEPS:
+                make_gain(0)
+            if i >= 1:
+                leaky_relu(i - 1)
+                square(i - 1)
+            if i == 1 or i == 2:
+                make_noise_bias(i + 1, 1)
+            if i >= 2:
+                sum_pixels(i - 2, 1)
+            if i == pair_0_summed:
+                stats_out(0)
+            if i == pair_0_summed + 1:
+                stats_back(0)
+            if i >= 1:
+                sum_pixels(i - 1, 0)
+            if i == pair_0_summed + 1:
+                stats_rstd(0)
+            if i + 2 < STEPS:
+                conv(i + 2)
+        make_mean_term(0)
+        make_shift(0)
+        sum_pixels(STEPS - 1, 1)
+        stats_out(1)
+
+        for ch in range(CHUNKS):
+            scale_y(0, ch)
+        turn_out(0, 0)
+        out_copy(0, 0, 0)
+        out_copy(0, 0, 1)
+        store(0, 0, 0, CHUNK_PIX)
+        turn_out(0, 1)
+        stats_back(1)
+        out_copy(0, 1, 0)
+        stats_rstd(1)
+        out_copy(0, 1, 1)
+        store(0, 1, 0, CHUNK_PIX)
+        make_gain(1)
+        make_mean_term(1)
+        make_shift(1)
+        for ch in range(CHUNKS - 1):
+            scale_y(1, ch)
+        for ch in range(2, CHUNKS):
+            turn_out(0, ch)
+            out_copy(0, ch, 0)
+            out_copy(0, ch, 1)
+            store(0, ch, 0, CHUNK_PIX)
+            if ch == 2:
+                scale_y(1, CHUNKS - 1)
+
+        for ch in range(CHUNKS):
+            turn_out(1, ch)
+            for half in range(2):
+                out_copy(1, ch, half)
+                if ch == CHUNKS - 1:
+                    store(1, ch, 2 * half, 2)
+            if ch < CHUNKS - 1:
+                store(1, ch, 0, CHUNK_PIX)

@@ -49,10 +49,10 @@ def tile_styleganlayerepilogue_kernel(
         ctx.enter_context(tc.manual_schedule())
 
         def work_bank(shape, dtype, name):
-            return psum.tile(shape, dtype, tag="work", bufs=5, name=name)
+            return psum.tile(shape, dtype, tag="work", bufs=6, name=name)
 
         def held_bank(shape, dtype, name):
-            return psum.tile(shape, dtype, tag="held", bufs=3, name=name)
+            return psum.tile(shape, dtype, tag="held", bufs=2, name=name)
 
         neg_eps = const.tile([P, 1], F32, name="neg_eps")
         nc.vector.memset(neg_eps[:], -EPS)
@@ -428,8 +428,9 @@ def tile_styleganlayerepilogue_kernel(
                 sum_pixels(i - 1, 0)
             if i == pair_0_summed + 1:
                 stats_rstd(0)
-            if i + 2 < STEPS:
+            if i % 2 == 0 and i + 2 < STEPS:
                 conv(i + 2)
+                conv(i + 3)
         make_mean_term(0)
         make_shift(0)
         sum_pixels(STEPS - 1, 1)

@@ -135,7 +135,7 @@ def tile_styleganlayerepilogue_kernel(
         w_scales = const.tile([P, NF], U8, name="w_scales", align_bytes=64)
 
         def w_interleave():
-            nc.scalar.copy(out=w_grouped[:], in_=w_raw[:].rearrange("p j o -> p o j"))
+            nc.vector.tensor_copy(out=w_grouped[:], in_=w_raw[:].rearrange("p j o -> p o j"))
 
         def w_quantize():
             nc.vector.quantize_mx(
@@ -381,10 +381,10 @@ def tile_styleganlayerepilogue_kernel(
         small_copies()
         make_noise_bias(0, 0)
         make_noise_bias(1, 0)
-        w_interleave()
         front(0, range(4))
         dlatents_transpose()
         front(1, range(2))
+        w_interleave()
         dlatents_copy()
         make_noise_bias(0, 1)
         front(1, range(2, 4))

@@ -60,9 +60,8 @@ def tile_styleganlayerepilogue_kernel(
         nc.vector.memset(vec_rows[:], 0.0)
 
         scale_bc = const.tile([P, K], F32, name="scale_bc")
-        nc.sync.dma_start(
-            out=scale_bc[:], in_=x_scale.rearrange("a b c k -> (a b c k)").partition_broadcast(P)
-        )
+        scale_cols = const.tile([P, PACK], F32, name="scale_cols")
+        nc.sync.dma_start(out=scale_cols[:], in_=x_scale.rearrange("a b c (n m) -> n (a b c m)", m=PACK))
         noise_sb = const.tile([P, PIX], BF16, name="noise_sb")
         nc.scalar.dma_start(out=noise_sb[:], in_=noise_map.rearrange("b h w o -> b (h w o)"))
         nc.scalar.dma_start(
@@ -89,15 +88,23 @@ def tile_styleganlayerepilogue_kernel(
         nc.sync.dma_start(out=dl_sb[:], in_=dlatents)
         nc.sync.dma_start(out=dense_w_sb[:], in_=dense_w.rearrange("(t p) n -> p t n", p=P))
 
-        ident_b = const.tile([P, P], BF16, name="ident_b")
-        make_identity(nc, ident_b[:])
         ident_f = const.tile([P, P], F32, name="ident_f")
         make_identity(nc, ident_f[:])
+        ident_b = const.tile([P, P], BF16, name="ident_b")
+        make_identity(nc, ident_b[:])
 
         def transpose_add(dst, src, start, stop):
             nc.tensor.matmul(out=dst, lhsT=src, rhs=ident_f[:], is_transpose=True, start=start, stop=stop)
 
         tiles = {}
+
+        def spread_scale():
+            scale_ps = work_bank([P, PACK, P], F32, "scale_ps")
+            for m in range(PACK):
+                nc.tensor.transpose(scale_ps[:, m, :], scale_cols[:, m : m + 1].to_broadcast([P, P]), ident_f[:])
+            nc.scalar.copy(
+                out=scale_bc[:].rearrange("p (n m) -> p n m", m=PACK), in_=scale_ps[:].rearrange("p m n -> p n m")
+            )
 
         vecs = const.tile([P, ROWS], F32, name="vecs")
         gamma_bias = const.tile([P, TILES], F32, name="gamma_bias")
@@ -377,6 +384,7 @@ def tile_styleganlayerepilogue_kernel(
             out_product(g, ch, 0)
             out_product(g, ch, 1)
 
+        spread_scale()
         small_transposes()
         small_copies()
         make_noise_bias(0, 0)

@@ -78,13 +78,19 @@ def tile_styleganlayerepilogue_kernel(
         w_raw = const.tile([P, PACK, NF], BF16, name="w_raw")
         dl_sb = const.tile([P, DENSE_KT * P], BF16, name="dl_sb")
         dense_w_sb = const.tile([P, DENSE_KT, 2 * NF], BF16, name="dense_w_sb")
+
+        def load_w(g):
+            cols = slice(g * 2 * P, (g + 1) * 2 * P)
+            nc.sync.dma_start(out=w_raw[:, :, cols], in_=conv_w.rearrange("(p j) o -> p j o", j=PACK)[:, :, cols])
+
+        load_w(0)
         x_byte_tiles = []
         for i in range(PIX // 2):
             x_byte_tile = const.tile([P, 2, K], U8, name="xbytes%d" % i)
             nc.sync.dma_start(out=x_byte_tile[:], in_=x_src[:, 2 * i : 2 * i + 2, :])
             x_byte_tiles.append(x_byte_tile)
             if 2 * (i + 1) == 2 * CHUNK_PIX:
-                nc.sync.dma_start(out=w_raw[:], in_=conv_w.rearrange("(p j) o -> p j o", j=PACK))
+                load_w(1)
         nc.sync.dma_start(out=dl_sb[:], in_=dlatents)
         nc.sync.dma_start(out=dense_w_sb[:], in_=dense_w.rearrange("(t p) n -> p t n", p=P))
 
@@ -123,9 +129,13 @@ def tile_styleganlayerepilogue_kernel(
                 tiles[("noise_rows", half)] = noise_rows
 
         def small_copies():
-            nc.vector.tensor_copy(out=vecs[:], in_=tiles["vecs_ps"][:, 0:ROWS])
-            nc.vector.tensor_scalar_add(
-                out=gamma_bias[:], in0=vecs[:, ROW_DENSE_GAMMA : ROW_DENSE_GAMMA + TILES], scalar1=1.0
+            nc.scalar.copy(out=vecs[:], in_=tiles["vecs_ps"][:, 0:ROWS])
+            nc.scalar.activation(
+                out=gamma_bias[:],
+                in_=tiles["vecs_ps"][:, ROW_DENSE_GAMMA : ROW_DENSE_GAMMA + TILES],
+                func=ACT.Copy,
+                bias=1.0,
+                scale=1.0,
             )
 
         def make_noise_bias(t, half):
@@ -141,8 +151,9 @@ def tile_styleganlayerepilogue_kernel(
         w_codes = const.tile([P, NF], U32, name="w_codes", align_bytes=64)
         w_scales = const.tile([P, NF], U8, name="w_scales", align_bytes=64)
 
-        def w_interleave():
-            nc.vector.tensor_copy(out=w_grouped[:], in_=w_raw[:].rearrange("p j o -> p o j"))
+        def w_interleave(g):
+            cols = slice(g * 2 * P, (g + 1) * 2 * P)
+            nc.vector.tensor_copy(out=w_grouped[:, cols, :], in_=w_raw[:, :, cols].rearrange("p j o -> p o j"))
 
         def w_quantize():
             nc.vector.quantize_mx(
@@ -384,6 +395,7 @@ def tile_styleganlayerepilogue_kernel(
             out_product(g, ch, 0)
             out_product(g, ch, 1)
 
+        w_interleave(0)
         spread_scale()
         small_transposes()
         small_copies()
@@ -392,7 +404,7 @@ def tile_styleganlayerepilogue_kernel(
         front(0, range(4))
         dlatents_transpose()
         front(1, range(2))
-        w_interleave()
+        w_interleave(1)
         dlatents_copy()
         make_noise_bias(0, 1)
         front(1, range(2, 4))
@@ -403,12 +415,12 @@ def tile_styleganlayerepilogue_kernel(
         front(3, range(2))
         w_quantize()
         x_quantize(0)
+        dense_matmul(1)
         front(3, range(2, 4))
+        dense_bias(1)
         x_quantize(1)
         x_quantize(2)
         conv(0)
-        dense_matmul(1)
-        dense_bias(1)
         conv(1)
         make_noise_bias(2, 0)
         make_noise_bias(3, 0)
@@ -432,13 +444,13 @@ def tile_styleganlayerepilogue_kernel(
                 stats_out(0)
             if i == pair_0_summed + 1:
                 stats_back(0)
+            if i % 2 == 0 and i + 2 < STEPS:
+                conv(i + 2)
+                conv(i + 3)
             if i >= 1:
                 sum_pixels(i - 1, 0)
             if i == pair_0_summed + 1:
                 stats_rstd(0)
-            if i % 2 == 0 and i + 2 < STEPS:
-                conv(i + 2)
-                conv(i + 3)
         make_mean_term(0)
         make_shift(0)
         sum_pixels(STEPS - 1, 1)

@@ -153,7 +153,10 @@ def tile_styleganlayerepilogue_kernel(
 
         def w_interleave(g):
             cols = slice(g * 2 * P, (g + 1) * 2 * P)
-            nc.vector.tensor_copy(out=w_grouped[:, cols, :], in_=w_raw[:, :, cols].rearrange("p j o -> p o j"))
+            if g == 0:
+                nc.vector.tensor_copy(out=w_grouped[:, cols, :], in_=w_raw[:, :, cols].rearrange("p j o -> p o j"))
+            else:
+                nc.scalar.copy(out=w_grouped[:, cols, :], in_=w_raw[:, :, cols].rearrange("p j o -> p o j"))
 
         def w_quantize():
             nc.vector.quantize_mx(
@@ -255,22 +258,27 @@ def tile_styleganlayerepilogue_kernel(
                 )
             tiles[("z", s)] = z
 
-        def leaky_relu(s):
-            y = const.tile([P, 2, CHUNK_PIX, P], F32, name="y%d" % s)
-            z = tiles[("z", s)][:].rearrange("p c n -> p (c n)")
+        def leaky_relu(s, first=0, count=2):
+            if first == 0:
+                tiles[("y", s)] = const.tile([P, 2, CHUNK_PIX, P], F32, name="y%d" % s)
+            z = tiles[("z", s)][:, first : first + count, :].rearrange("p c n -> p (c n)")
             nc.vector.scalar_tensor_tensor(
-                out=y[:].rearrange("p c x b -> p (c x b)"), in0=z, scalar=SLOPE, in1=z, op0=ALU.mult, op1=ALU.max
+                out=tiles[("y", s)][:, first : first + count, :, :].rearrange("p c x b -> p (c x b)"),
+                in0=z,
+                scalar=SLOPE,
+                in1=z,
+                op0=ALU.mult,
+                op1=ALU.max,
             )
-            tiles[("y", s)] = y
 
-        def square(s):
-            q = q_pool.tile([P, 2, CHUNK_PIX, P], F32, name="q")
+        def square(s, first=0, count=2):
+            if first == 0:
+                tiles[("q", s)] = q_pool.tile([P, 2, CHUNK_PIX, P], F32, name="q")
             nc.scalar.activation(
-                out=q[:].rearrange("p c x b -> p (c x b)"),
-                in_=tiles[("y", s)][:].rearrange("p c x b -> p (c x b)"),
+                out=tiles[("q", s)][:, first : first + count, :, :].rearrange("p c x b -> p (c x b)"),
+                in_=tiles[("y", s)][:, first : first + count, :, :].rearrange("p c x b -> p (c x b)"),
                 func=ACT.Square,
             )
-            tiles[("q", s)] = q
 
         def sum_pixels(s, power):
             g, ch = s // CHUNKS, s % CHUNKS
@@ -342,15 +350,15 @@ def tile_styleganlayerepilogue_kernel(
 
         out_v = out.rearrange("b h w o -> b (h w) o")
 
-        def scale_y(g, ch):
-            ya = ya_pool.tile([P, 2, CHUNK_PIX, P], F32, name="ya")
+        def scale_y(g, ch, first=0, count=CHUNK_PIX):
+            if first == 0:
+                tiles[("ya", g, ch)] = ya_pool.tile([P, 2, CHUNK_PIX, P], F32, name="ya")
             nc.vector.tensor_tensor(
-                out=ya[:],
-                in0=tiles[("y", g * CHUNKS + ch)][:],
-                in1=tiles[("gain", g)][:].to_broadcast([P, 2, CHUNK_PIX, P]),
+                out=tiles[("ya", g, ch)][:, :, first : first + count, :],
+                in0=tiles[("y", g * CHUNKS + ch)][:, :, first : first + count, :],
+                in1=tiles[("gain", g)][:].to_broadcast([P, 2, count, P]),
                 op=ALU.mult,
             )
-            tiles[("ya", g, ch)] = ya
 
         def out_shift(g, ch, half):
             out_ps = work_bank([P, 2, 2, P], F32, "out_ps")
@@ -415,13 +423,13 @@ def tile_styleganlayerepilogue_kernel(
         front(3, range(2))
         w_quantize()
         x_quantize(0)
-        dense_matmul(1)
+        conv(0)
         front(3, range(2, 4))
-        dense_bias(1)
         x_quantize(1)
         x_quantize(2)
-        conv(0)
         conv(1)
+        dense_matmul(1)
+        dense_bias(1)
         make_noise_bias(2, 0)
         make_noise_bias(3, 0)
 
@@ -433,9 +441,13 @@ def tile_styleganlayerepilogue_kernel(
                 x_quantize(CHUNKS - 1)
             if i == STEPS:
                 make_gain(0)
-            if i >= 1:
+            if 1 <= i < STEPS:
                 leaky_relu(i - 1)
                 square(i - 1)
+            if i == STEPS:
+                for c in range(2):
+                    leaky_relu(i - 1, c, 1)
+                    square(i - 1, c, 1)
             if i == 1 or i == 2:
                 make_noise_bias(i + 1, 1)
             if i >= 2:
@@ -479,7 +491,8 @@ def tile_styleganlayerepilogue_kernel(
             out_copy(0, ch, 1)
             store(0, ch, 0, CHUNK_PIX)
             if ch == 2:
-                scale_y(1, CHUNKS - 1)
+                scale_y(1, CHUNKS - 1, 0, 2)
+                scale_y(1, CHUNKS - 1, 2, 2)
 
         for ch in range(CHUNKS):
             turn_out(1, ch)

@@ -428,8 +428,6 @@ def tile_styleganlayerepilogue_kernel(
         x_quantize(1)
         x_quantize(2)
         conv(1)
-        dense_matmul(1)
-        dense_bias(1)
         make_noise_bias(2, 0)
         make_noise_bias(3, 0)
 
@@ -459,6 +457,9 @@ def tile_styleganlayerepilogue_kernel(
             if i % 2 == 0 and i + 2 < STEPS:
                 conv(i + 2)
                 conv(i + 3)
+            if i == 0:
+                dense_matmul(1)
+                dense_bias(1)
             if i >= 1:
                 sum_pixels(i - 1, 0)
             if i == pair_0_summed + 1:
@@ -471,13 +472,13 @@ def tile_styleganlayerepilogue_kernel(
         for ch in range(CHUNKS):
             scale_y(0, ch)
         turn_out(0, 0)
+        stats_back(1)
         out_copy(0, 0, 0)
+        stats_rstd(1)
         out_copy(0, 0, 1)
         store(0, 0, 0, CHUNK_PIX)
         turn_out(0, 1)
-        stats_back(1)
         out_copy(0, 1, 0)
-        stats_rstd(1)
         out_copy(0, 1, 1)
         store(0, 1, 0, CHUNK_PIX)
         make_gain(1)

@@ -474,13 +474,14 @@ def tile_styleganlayerepilogue_kernel(
         turn_out(0, 0)
         stats_back(1)
         out_copy(0, 0, 0)
+        store(0, 0, 0, 2)
         stats_rstd(1)
         out_copy(0, 0, 1)
-        store(0, 0, 0, CHUNK_PIX)
+        store(0, 0, 2, 2)
         turn_out(0, 1)
-        out_copy(0, 1, 0)
-        out_copy(0, 1, 1)
-        store(0, 1, 0, CHUNK_PIX)
+        for half in range(2):
+            out_copy(0, 1, half)
+            store(0, 1, 2 * half, 2)
         make_gain(1)
         make_mean_term(1)
         make_shift(1)
@@ -488,9 +489,9 @@ def tile_styleganlayerepilogue_kernel(
             scale_y(1, ch)
         for ch in range(2, CHUNKS):
             turn_out(0, ch)
-            out_copy(0, ch, 0)
-            out_copy(0, ch, 1)
-            store(0, ch, 0, CHUNK_PIX)
+            for half in range(2):
+                out_copy(0, ch, half)
+                store(0, ch, 2 * half, 2)
             if ch == 2:
                 scale_y(1, CHUNKS - 1, 0, 2)
                 scale_y(1, CHUNKS - 1, 2, 2)
@@ -499,7 +500,4 @@ def tile_styleganlayerepilogue_kernel(
             turn_out(1, ch)
             for half in range(2):
                 out_copy(1, ch, half)
-                if ch == CHUNKS - 1:
-                    store(1, ch, 2 * half, 2)
-            if ch < CHUNKS - 1:
-                store(1, ch, 0, CHUNK_PIX)
+                store(1, ch, 2 * half, 2)

@@ -26,6 +26,7 @@ STEPS = PAIRS * CHUNKS
 HALF_PIX = PIX // 2
 DENSE_KT = 4
 ROW_NOISE_WEIGHT, ROW_BIAS, ROW_DENSE_GAMMA, ROW_DENSE_BETA, ROWS = 0, 4, 8, 12, 16
+SHIFT_ON_VECTOR = (1, 3)
 EPS = 1e-8
 SLOPE = 0.2
 
@@ -342,9 +343,9 @@ def tile_styleganlayerepilogue_kernel(
             tiles[("mean_term", g)] = mean_term
 
         def make_shift(g):
-            shift = stat_pool.tile([P, 2, P], F32, name="shift")
+            shift = stat_pool.tile([P, 2, 1, P], F32, name="shift")
             nc.vector.tensor_tensor(
-                out=shift[:], in0=tiles[("mean_term", g)][:], in1=beta[:, 2 * g : 2 * g + 2, :], op=ALU.add
+                out=shift[:, :, 0, :], in0=tiles[("mean_term", g)][:], in1=beta[:, 2 * g : 2 * g + 2, :], op=ALU.add
             )
             tiles[("shift", g)] = shift
 
@@ -360,20 +361,29 @@ def tile_styleganlayerepilogue_kernel(
                 op=ALU.mult,
             )
 
+        def add_shift(g, ch, first, count):
+            ya = tiles[("ya", g, ch)][:, :, first : first + count, :]
+            nc.vector.tensor_tensor(
+                out=ya, in0=ya, in1=tiles[("shift", g)][:].to_broadcast([P, 2, count, P]), op=ALU.add
+            )
+
         def out_shift(g, ch, half):
             out_ps = work_bank([P, 2, 2, P], F32, "out_ps")
             for x in range(2):
                 for c in range(2):
-                    transpose_add(out_ps[:, x, c, :], tiles[("shift", g)][:, c, :], x == 0 and c == 0, False)
+                    transpose_add(out_ps[:, x, c, :], tiles[("shift", g)][:, c, 0, :], x == 0 and c == 0, False)
             tiles[("out_ps", g, ch, half)] = out_ps
 
         def out_product(g, ch, half):
+            opens = (g, ch) == SHIFT_ON_VECTOR
+            if opens:
+                tiles[("out_ps", g, ch, half)] = work_bank([P, 2, 2, P], F32, "out_ps")
             for x in range(2):
                 for c in range(2):
                     transpose_add(
                         tiles[("out_ps", g, ch, half)][:, x, c, :],
                         tiles[("ya", g, ch)][:, c, 2 * half + x, :],
-                        False,
+                        opens and x == 0 and c == 0,
                         x == 1 and c == 1,
                     )
 
@@ -398,8 +408,9 @@ def tile_styleganlayerepilogue_kernel(
                     x_group(ch, x // 2)
 
         def turn_out(g, ch):
-            out_shift(g, ch, 0)
-            out_shift(g, ch, 1)
+            if (g, ch) != SHIFT_ON_VECTOR:
+                out_shift(g, ch, 0)
+                out_shift(g, ch, 1)
             out_product(g, ch, 0)
             out_product(g, ch, 1)
 
@@ -495,6 +506,8 @@ def tile_styleganlayerepilogue_kernel(
             if ch == 2:
                 scale_y(1, CHUNKS - 1, 0, 2)
                 scale_y(1, CHUNKS - 1, 2, 2)
+                add_shift(1, CHUNKS - 1, 0, 2)
+                add_shift(1, CHUNKS - 1, 2, 2)
 
         for ch in range(CHUNKS):
             turn_out(1, ch)

from contextlib import ExitStack

import concourse.mybir as mybir
from concourse.masks import make_identity

F32 = mybir.dt.float32
BF16 = mybir.dt.bfloat16
U32 = mybir.dt.uint32
U8 = mybir.dt.uint8
FP8 = mybir.dt.float8_e4m3fn
FP8X4 = mybir.dt.float8_e4m3fn_x4
ALU = mybir.AluOpType
ACT = mybir.ActivationFunctionType

P = 128
PIX = 16
K = 512
PACK = 4
NF = 512
TILES = NF // P
PAIRS = TILES // 2
CHUNK_PIX = 4
CHUNKS = PIX // CHUNK_PIX
CHUNK = CHUNK_PIX * P
STEPS = PAIRS * CHUNKS
HALF_PIX = PIX // 2
DENSE_KT = 4
ROW_NOISE_WEIGHT, ROW_BIAS, ROW_DENSE_GAMMA, ROW_DENSE_BETA, ROWS = 0, 4, 8, 12, 16
SHIFT_ON_VECTOR = (1, 3)
EPS = 1e-8
SLOPE = 0.2

FLOPS = 2 * P * PIX * K * NF + 2 * P * 512 * 2 * NF


def tile_styleganlayerepilogue_kernel(
    tc, x_bytes, x_scale, dlatents, noise_map, conv_w, noise_weight, bias, dense_w, dense_b, out
):
    nc = tc.nc
    with ExitStack() as ctx:
        const = ctx.enter_context(tc.tile_pool(name="const", bufs=1))
        xs_pool = ctx.enter_context(tc.tile_pool(name="xs_pool", bufs=6))
        grouped_pool = ctx.enter_context(tc.tile_pool(name="grouped_pool", bufs=CHUNKS))
        z_pool = ctx.enter_context(tc.tile_pool(name="z_pool", bufs=3))
        q_pool = ctx.enter_context(tc.tile_pool(name="q_pool", bufs=3))
        stat_pool = ctx.enter_context(tc.tile_pool(name="stat_pool", bufs=PAIRS))
        ya_pool = ctx.enter_context(tc.tile_pool(name="ya_pool", bufs=5))
        o_pool = ctx.enter_context(tc.tile_pool(name="o_pool", bufs=6))
        psum = ctx.enter_context(tc.psum_pool(name="psum", bufs=2))
        ctx.enter_context(tc.manual_schedule())

        def work_bank(shape, dtype, name):
            return psum.tile(shape, dtype, tag="work", bufs=6, name=name)

        def held_bank(shape, dtype, name):
            return psum.tile(shape, dtype, tag="held", bufs=2, name=name)

        neg_eps = const.tile([P, 1], F32, name="neg_eps")
        nc.vector.memset(neg_eps[:], -EPS)
        vec_rows = const.tile([P, P], BF16, name="vec_rows")
        nc.vector.memset(vec_rows[:], 0.0)

        scale_bc = const.tile([P, K], F32, name="scale_bc")
        scale_cols = const.tile([P, PACK], F32, name="scale_cols")
        nc.sync.dma_start(out=scale_cols[:], in_=x_scale.rearrange("a b c (n m) -> n (a b c m)", m=PACK))
        noise_sb = const.tile([P, PIX], BF16, name="noise_sb")
        nc.scalar.dma_start(out=noise_sb[:], in_=noise_map.rearrange("b h w o -> b (h w o)"))
        nc.scalar.dma_start(
            out=vec_rows[ROW_NOISE_WEIGHT:ROW_BIAS, :], in_=noise_weight.rearrange("a b c (t p) -> (a b c t) p", p=P)
        )
        nc.scalar.dma_start(
            out=vec_rows[ROW_BIAS:ROW_DENSE_GAMMA, :], in_=bias.rearrange("a b c (t p) -> (a b c t) p", p=P)
        )
        nc.scalar.dma_start(out=vec_rows[ROW_DENSE_GAMMA:ROWS, :], in_=dense_b.rearrange("(t p) -> t p", p=P))
        warm = const.tile([P, 1], F32, name="warm")
        nc.scalar.activation(out=warm[:], in_=neg_eps[:], func=ACT.Abs_reciprocal_sqrt)

        x_src = x_bytes.rearrange("b h w k -> b (h w) k")
        w_raw = const.tile([P, PACK, NF], BF16, name="w_raw")
        dl_sb = const.tile([P, DENSE_KT * P], BF16, name="dl_sb")
        dense_w_sb = const.tile([P, DENSE_KT, 2 * NF], BF16, name="dense_w_sb")

        def load_w(g):
            cols = slice(g * 2 * P, (g + 1) * 2 * P)
            nc.sync.dma_start(out=w_raw[:, :, cols], in_=conv_w.rearrange("(p j) o -> p j o", j=PACK)[:, :, cols])

        load_w(0)
        x_byte_tiles = []
        for i in range(PIX // 2):
            x_byte_tile = const.tile([P, 2, K], U8, name="xbytes%d" % i)
            nc.sync.dma_start(out=x_byte_tile[:], in_=x_src[:, 2 * i : 2 * i + 2, :])
            x_byte_tiles.append(x_byte_tile)
            if 2 * (i + 1) == 2 * CHUNK_PIX:
                load_w(1)
        nc.sync.dma_start(out=dl_sb[:], in_=dlatents)
        nc.sync.dma_start(out=dense_w_sb[:], in_=dense_w.rearrange("(t p) n -> p t n", p=P))

        ident_f = const.tile([P, P], F32, name="ident_f")
        make_identity(nc, ident_f[:])
        ident_b = const.tile([P, P], BF16, name="ident_b")
        make_identity(nc, ident_b[:])

        def transpose_add(dst, src, start, stop):
            nc.tensor.matmul(out=dst, lhsT=src, rhs=ident_f[:], is_transpose=True, start=start, stop=stop)

        tiles = {}

        def spread_scale():
            scale_ps = work_bank([P, PACK, P], F32, "scale_ps")
            for m in range(PACK):
                nc.tensor.transpose(scale_ps[:, m, :], scale_cols[:, m : m + 1].to_broadcast([P, P]), ident_f[:])
            nc.scalar.copy(
                out=scale_bc[:].rearrange("p (n m) -> p n m", m=PACK), in_=scale_ps[:].rearrange("p m n -> p n m")
            )

        vecs = const.tile([P, ROWS], F32, name="vecs")
        gamma_bias = const.tile([P, TILES], F32, name="gamma_bias")
        noise_bias = [const.tile([P, PIX * P], F32, name="noise_bias%d" % t) for t in range(TILES)]

        def small_transposes():
            tiles["vecs_ps"] = work_bank([P, P], BF16, "vecs_ps")
            nc.tensor.transpose(tiles["vecs_ps"][:], vec_rows[:], ident_b[:])
            for half in range(2):
                noise_rows = held_bank([P, HALF_PIX * P], BF16, "noise_rows")
                for x in range(HALF_PIX):
                    pix = HALF_PIX * half + x
                    nc.tensor.transpose(
                        noise_rows[:, x * P : (x + 1) * P], noise_sb[:, pix : pix + 1].to_broadcast([P, P]), ident_b[:]
                    )
                tiles[("noise_rows", half)] = noise_rows

        def small_copies():
            nc.scalar.copy(out=vecs[:], in_=tiles["vecs_ps"][:, 0:ROWS])
            nc.scalar.activation(
                out=gamma_bias[:],
                in_=tiles["vecs_ps"][:, ROW_DENSE_GAMMA : ROW_DENSE_GAMMA + TILES],
                func=ACT.Copy,
                bias=1.0,
                scale=1.0,
            )

        def make_noise_bias(t, half):
            nc.scalar.activation(
                out=noise_bias[t][:, half * HALF_PIX * P : (half + 1) * HALF_PIX * P],
                in_=tiles[("noise_rows", half)][:],
                func=ACT.Identity,
                bias=vecs[:, ROW_BIAS + t : ROW_BIAS + t + 1],
                scale=vecs[:, ROW_NOISE_WEIGHT + t : ROW_NOISE_WEIGHT + t + 1],
            )

        w_grouped = const.tile([P, NF, PACK], BF16, name="w_grouped", align_bytes=64)
        w_codes = const.tile([P, NF], U32, name="w_codes", align_bytes=64)
        w_scales = const.tile([P, NF], U8, name="w_scales", align_bytes=64)

        def w_interleave(g):
            cols = slice(g * 2 * P, (g + 1) * 2 * P)
            if g == 0:
                nc.vector.tensor_copy(out=w_grouped[:, cols, :], in_=w_raw[:, :, cols].rearrange("p j o -> p o j"))
            else:
                nc.scalar.copy(out=w_grouped[:, cols, :], in_=w_raw[:, :, cols].rearrange("p j o -> p o j"))

        def w_quantize():
            nc.vector.quantize_mx(
                out=w_codes[:].bitcast(FP8X4), scales=w_scales[:], in_=w_grouped[:].rearrange("p o j -> p (o j)")
            )

        def widen(ch, x):
            pix = ch * CHUNK_PIX + x
            xs = xs_pool.tile([P, K], BF16, name="xs")
            nc.vector.tensor_tensor(
                out=xs[:], in0=x_byte_tiles[pix // 2][:, pix % 2, :].bitcast(FP8), in1=scale_bc[:], op=ALU.mult
            )
            tiles[("xs", ch, x)] = xs

        def x_transpose(ch, x):
            if x % 2 == 0:
                tiles[("xt", ch, x // 2)] = work_bank([P, 2, 2, P], F32, "xt")
            words = tiles[("xs", ch, x)][:].bitcast(F32)
            for u in range(2):
                nc.tensor.transpose(tiles[("xt", ch, x // 2)][:, x % 2, u, :], words[:, u : K // 2 : 2], ident_f[:])

        def x_group(ch, half):
            if half == 0:
                tiles[("grouped", ch)] = grouped_pool.tile([P, CHUNK * PACK], BF16, name="grouped", align_bytes=64)
            words = tiles[("grouped", ch)][:].bitcast(F32)
            nc.scalar.copy(
                out=words[:, half * CHUNK : (half + 1) * CHUNK].rearrange("p (x b u) -> p x b u", x=2, u=2),
                in_=tiles[("xt", ch, half)][:].rearrange("p x u b -> p x b u"),
            )

        def x_quantize(ch):
            codes = const.tile([P, CHUNK], U32, name="x_codes%d" % ch, align_bytes=64)
            scales = const.tile([P, CHUNK], U8, name="x_scales%d" % ch, align_bytes=64)
            nc.vector.quantize_mx(out=codes[:].bitcast(FP8X4), scales=scales[:], in_=tiles[("grouped", ch)][:])
            tiles[("x_codes", ch)] = codes
            tiles[("x_scales", ch)] = scales

        dlatents_t = const.tile([P, DENSE_KT, P], BF16, name="dlatents_t")
        gamma1 = const.tile([P, TILES, P], F32, name="gamma1")
        beta = const.tile([P, TILES, P], F32, name="beta")

        def dlatents_transpose():
            tiles["dlatents_ps"] = work_bank([P, DENSE_KT, P], BF16, "dlatents_ps")
            for kt in range(DENSE_KT):
                nc.tensor.transpose(tiles["dlatents_ps"][:, kt, :], dl_sb[:, kt * P : (kt + 1) * P], ident_b[:])

        def dlatents_copy():
            nc.scalar.copy(out=dlatents_t[:], in_=tiles["dlatents_ps"][:])

        def dense_matmul(part):
            dense_ps = work_bank([P, TILES, P], F32, "dense_ps")
            for t in range(TILES):
                col = (part * TILES + t) * P
                for kt in range(DENSE_KT):
                    nc.tensor.matmul(
                        out=dense_ps[:, t, :],
                        lhsT=dense_w_sb[:, kt, col : col + P],
                        rhs=dlatents_t[:, kt, :],
                        start=(kt == 0),
                        stop=(kt == DENSE_KT - 1),
                    )
            tiles[("dense_ps", part)] = dense_ps

        def dense_bias(part):
            for t in range(TILES):
                nc.scalar.activation(
                    out=(gamma1 if part == 0 else beta)[:, t, :],
                    in_=tiles[("dense_ps", part)][:, t, :],
                    func=ACT.Identity,
                    bias=(gamma_bias if part == 0 else vecs[:, ROW_DENSE_BETA:ROWS])[:, t : t + 1],
                    scale=1.0,
                )

        def conv(s):
            g, ch = s // CHUNKS, s % CHUNKS
            for c in range(2):
                t = 2 * g + c
                acc = work_bank([P, CHUNK], F32, "acc")
                nc.tensor.matmul_mx(
                    out=acc[:],
                    lhsT=w_codes[:, t * P : (t + 1) * P].bitcast(FP8X4),
                    lhsT_scale=w_scales[:, t * P : (t + 1) * P],
                    rhs=tiles[("x_codes", ch)][:].bitcast(FP8X4),
                    rhs_scale=tiles[("x_scales", ch)][:],
                    start=True,
                    stop=True,
                )
                tiles[("acc", s, c)] = acc

        def add_noise(s):
            g, ch = s // CHUNKS, s % CHUNKS
            z = z_pool.tile([P, 2, CHUNK], F32, name="z")
            for c in range(2):
                nc.vector.tensor_tensor(
                    out=z[:, c, :],
                    in0=tiles[("acc", s, c)][:],
                    in1=noise_bias[2 * g + c][:, ch * CHUNK : (ch + 1) * CHUNK],
                    op=ALU.add,
                )
            tiles[("z", s)] = z

        def leaky_relu(s, first=0, count=2):
            if first == 0:
                tiles[("y", s)] = const.tile([P, 2, CHUNK_PIX, P], F32, name="y%d" % s)
            z = tiles[("z", s)][:, first : first + count, :].rearrange("p c n -> p (c n)")
            nc.vector.scalar_tensor_tensor(
                out=tiles[("y", s)][:, first : first + count, :, :].rearrange("p c x b -> p (c x b)"),
                in0=z,
                scalar=SLOPE,
                in1=z,
                op0=ALU.mult,
                op1=ALU.max,
            )

        def square(s, first=0, count=2):
            if first == 0:
                tiles[("q", s)] = q_pool.tile([P, 2, CHUNK_PIX, P], F32, name="q")
            nc.scalar.activation(
                out=tiles[("q", s)][:, first : first + count, :, :].rearrange("p c x b -> p (c x b)"),
                in_=tiles[("y", s)][:, first : first + count, :, :].rearrange("p c x b -> p (c x b)"),
                func=ACT.Square,
            )

        def sum_pixels(s, power):
            g, ch = s // CHUNKS, s % CHUNKS
            if ch == 0 and power == 0:
                tiles[("sums", g)] = held_bank([P, 2, 2, P], F32, "sums")
            src = tiles[("y" if power == 0 else "q", s)]
            for c in range(2):
                for x in range(CHUNK_PIX):
                    transpose_add(
                        tiles[("sums", g)][:, c, power, :],
                        src[:, c, x, :],
                        ch == 0 and power == 0 and c == 0 and x == 0,
                        ch == CHUNKS - 1 and power == 1 and c == 1 and x == CHUNK_PIX - 1,
                    )

        def stats_out(g):
            sums = tiles[("sums", g)]
            parts = stat_pool.tile([P, 2, 3, P], F32, name="parts")
            nc.scalar.copy(out=parts[:, :, 0, :], in_=sums[:, :, 0, :])
            nc.scalar.activation(out=parts[:, :, 1, :], in_=sums[:, :, 1, :], func=ACT.Copy, scale=-1.0 / PIX)
            nc.scalar.activation(out=parts[:, :, 2, :], in_=sums[:, :, 0, :], func=ACT.Square, scale=1.0 / PIX)
            tiles[("parts", g)] = parts

        def stats_back(g):
            parts = tiles[("parts", g)]
            stats = held_bank([P, 2, 2, P], F32, "stats")
            for c in range(2):
                transpose_add(stats[:, c, 0, :], parts[:, c, 0, :], c == 0, False)
                transpose_add(stats[:, c, 1, :], parts[:, c, 1, :], False, False)
                transpose_add(stats[:, c, 1, :], parts[:, c, 2, :], False, c == 1)
            tiles[("stats", g)] = stats

        def stats_rstd(g):
            rstd = stat_pool.tile([P, 2, P], F32, name="rstd")
            nc.scalar.activation(
                out=rstd[:],
                in_=tiles[("stats", g)][:, :, 1, :],
                func=ACT.Abs_reciprocal_sqrt,
                bias=neg_eps[:],
                scale=1.0,
            )
            tiles[("rstd", g)] = rstd

        def make_gain(g):
            gain = stat_pool.tile([P, 2, 1, P], F32, name="gain")
            nc.vector.tensor_tensor(
                out=gain[:, :, 0, :], in0=gamma1[:, 2 * g : 2 * g + 2, :], in1=tiles[("rstd", g)][:], op=ALU.mult
            )
            tiles[("gain", g)] = gain

        def make_mean_term(g):
            mean_term = stat_pool.tile([P, 2, P], F32, name="mean_term")
            nc.vector.scalar_tensor_tensor(
                out=mean_term[:],
                in0=tiles[("stats", g)][:, :, 0, :],
                scalar=-1.0 / PIX,
                in1=tiles[("gain", g)][:, :, 0, :],
                op0=ALU.mult,
                op1=ALU.mult,
            )
            tiles[("mean_term", g)] = mean_term

        def make_shift(g):
            shift = stat_pool.tile([P, 2, 1, P], F32, name="shift")
            nc.vector.tensor_tensor(
                out=shift[:, :, 0, :], in0=tiles[("mean_term", g)][:], in1=beta[:, 2 * g : 2 * g + 2, :], op=ALU.add
            )
            tiles[("shift", g)] = shift

        out_v = out.rearrange("b h w o -> b (h w) o")

        def scale_y(g, ch, first=0, count=CHUNK_PIX):
            if first == 0:
                tiles[("ya", g, ch)] = ya_pool.tile([P, 2, CHUNK_PIX, P], F32, name="ya")
            nc.vector.tensor_tensor(
                out=tiles[("ya", g, ch)][:, :, first : first + count, :],
                in0=tiles[("y", g * CHUNKS + ch)][:, :, first : first + count, :],
                in1=tiles[("gain", g)][:].to_broadcast([P, 2, count, P]),
                op=ALU.mult,
            )

        def add_shift(g, ch, first, count):
            ya = tiles[("ya", g, ch)][:, :, first : first + count, :]
            nc.vector.tensor_tensor(
                out=ya, in0=ya, in1=tiles[("shift", g)][:].to_broadcast([P, 2, count, P]), op=ALU.add
            )

        def out_shift(g, ch, half):
            out_ps = work_bank([P, 2, 2, P], F32, "out_ps")
            for x in range(2):
                for c in range(2):
                    transpose_add(out_ps[:, x, c, :], tiles[("shift", g)][:, c, 0, :], x == 0 and c == 0, False)
            tiles[("out_ps", g, ch, half)] = out_ps

        def out_product(g, ch, half):
            opens = (g, ch) == SHIFT_ON_VECTOR
            if opens:
                tiles[("out_ps", g, ch, half)] = work_bank([P, 2, 2, P], F32, "out_ps")
            for x in range(2):
                for c in range(2):
                    transpose_add(
                        tiles[("out_ps", g, ch, half)][:, x, c, :],
                        tiles[("ya", g, ch)][:, c, 2 * half + x, :],
                        opens and x == 0 and c == 0,
                        x == 1 and c == 1,
                    )

        def out_copy(g, ch, half):
            if half == 0:
                tiles[("out_sb", g, ch)] = o_pool.tile([P, CHUNK_PIX, 2, P], F32, name="out_sb")
            nc.scalar.copy(
                out=tiles[("out_sb", g, ch)][:, 2 * half : 2 * half + 2, :, :], in_=tiles[("out_ps", g, ch, half)][:]
            )

        def store(g, ch, first, count):
            nc.sync.dma_start(
                out=out_v[:, ch * CHUNK_PIX + first : ch * CHUNK_PIX + first + count, g * 2 * P : (g + 1) * 2 * P],
                in_=tiles[("out_sb", g, ch)][:, first : first + count, :, :].rearrange("p x c o -> p x (c o)"),
            )

        def front(ch, pixels):
            for x in pixels:
                widen(ch, x)
                x_transpose(ch, x)
                if x % 2 == 1:
                    x_group(ch, x // 2)

        def turn_out(g, ch):
            if (g, ch) != SHIFT_ON_VECTOR:
                out_shift(g, ch, 0)
                out_shift(g, ch, 1)
            out_product(g, ch, 0)
            out_product(g, ch, 1)

        w_interleave(0)
        spread_scale()
        small_transposes()
        small_copies()
        make_noise_bias(0, 0)
        make_noise_bias(1, 0)
        front(0, range(4))
        dlatents_transpose()
        front(1, range(2))
        w_interleave(1)
        dlatents_copy()
        make_noise_bias(0, 1)
        front(1, range(2, 4))
        make_noise_bias(1, 1)
        front(2, range(4))
        dense_matmul(0)
        dense_bias(0)
        front(3, range(2))
        w_quantize()
        x_quantize(0)
        conv(0)
        front(3, range(2, 4))
        x_quantize(1)
        x_quantize(2)
        conv(1)
        make_noise_bias(2, 0)
        make_noise_bias(3, 0)

        pair_0_summed = CHUNKS + 1
        for i in range(STEPS + 1):
            if i < STEPS:
                add_noise(i)
            if i == 0:
                x_quantize(CHUNKS - 1)
            if i == STEPS:
                make_gain(0)
            if 1 <= i < STEPS:
                leaky_relu(i - 1)
                square(i - 1)
            if i == STEPS:
                for c in range(2):
                    leaky_relu(i - 1, c, 1)
                    square(i - 1, c, 1)
            if i == 1 or i == 2:
                make_noise_bias(i + 1, 1)
            if i >= 2:
                sum_pixels(i - 2, 1)
            if i == pair_0_summed:
                stats_out(0)
            if i == pair_0_summed + 1:
                stats_back(0)
            if i % 2 == 0 and i + 2 < STEPS:
                conv(i + 2)
                conv(i + 3)
            if i == 0:
                dense_matmul(1)
                dense_bias(1)
            if i >= 1:
                sum_pixels(i - 1, 0)
            if i == pair_0_summed + 1:
                stats_rstd(0)
        make_mean_term(0)
        make_shift(0)
        sum_pixels(STEPS - 1, 1)
        stats_out(1)

        for ch in range(CHUNKS):
            scale_y(0, ch)
        turn_out(0, 0)
        stats_back(1)
        out_copy(0, 0, 0)
        store(0, 0, 0, 2)
        stats_rstd(1)
        out_copy(0, 0, 1)
        store(0, 0, 2, 2)
        turn_out(0, 1)
        for half in range(2):
            out_copy(0, 1, half)
            store(0, 1, 2 * half, 2)
        make_gain(1)
        make_mean_term(1)
        make_shift(1)
        for ch in range(CHUNKS - 1):
            scale_y(1, ch)
        for ch in range(2, CHUNKS):
            turn_out(0, ch)
            for half in range(2):
                out_copy(0, ch, half)
                store(0, ch, 2 * half, 2)
            if ch == 2:
                scale_y(1, CHUNKS - 1, 0, 2)
                scale_y(1, CHUNKS - 1, 2, 2)
                add_shift(1, CHUNKS - 1, 0, 2)
                add_shift(1, CHUNKS - 1, 2, 2)

        for ch in range(CHUNKS):
            turn_out(1, ch)
            for half in range(2):
                out_copy(1, ch, half)
                store(1, ch, 2 * half, 2)
